import numpy as np
import ml_dtypes


def mxq(x, axis, fmt="e4m3"):
    dtype, down = {"e4m3": (ml_dtypes.float8_e4m3fn, 7), "e5m2": (ml_dtypes.float8_e5m2, 14)}[fmt]
    v = np.moveaxis(np.asarray(x, np.float32).astype(ml_dtypes.bfloat16).astype(np.float64), axis, -1)
    blocks = v.reshape(v.shape[:-1] + (-1, 32))
    amax = np.abs(blocks).max(-1, keepdims=True)
    byte = np.maximum(np.where(amax > 0, np.frexp(amax)[1] - 1 + 127, 0) - down, 1)
    scale = np.exp2(byte - 127.0)
    codes = (blocks / scale).astype(np.float32).astype(dtype).astype(np.float64)
    return np.moveaxis((codes * scale).reshape(v.shape), -1, axis)


WIDE = False


def mx_kscale(k):
    if not WIDE:
        return np.ones(k)
    levels = np.array([10, -10, 5, -5, 0])
    a = np.random.permutation(np.resize(levels, k // 512 * 4)).reshape(k // 512, 4)
    idx = np.arange(k)
    return np.exp2(a[idx // 512, idx % 128 // 32])


BF16 = ml_dtypes.bfloat16


def bf(x):
    return np.asarray(x, np.float32).astype(BF16)


def f64(x):
    return np.asarray(x).astype(np.float64)


E2M1 = np.array([0.0, 0.5, 1.0, 1.5, 2.0, 3.0, 4.0, 6.0, -0.0, -0.5, -1.0, -1.5, -2.0, -3.0, -4.0, -6.0])


def pack_weight(w, fmt):
    k, n = w.shape
    w = f64(bf(w)).reshape(k // 32, 32, n)
    amax = np.abs(w).max(1)
    if fmt == "e4m3":
        byte = np.frexp(amax)[1] - 1 + 127 - 7
    else:
        mant, ex = np.frexp(amax / 6.0)
        byte = np.where(mant > 0.5, ex, ex - 1) + 127
    byte = np.clip(np.where(amax > 0, byte, 1), 1, 254)
    scaled = (w * np.exp2(127.0 - byte)[:, None, :]).reshape(k, n).astype(np.float32)
    by_word = np.ascontiguousarray(scaled.reshape(k // 512, 128, 4, n).transpose(0, 1, 3, 2))
    if fmt == "e4m3":
        words = by_word.astype(ml_dtypes.float8_e4m3fn).view(np.uint8)
    else:
        c = by_word.astype(ml_dtypes.float4_e2m1fn).view(np.uint8) & 0xF
        words = c[..., 0::2] | (c[..., 1::2] << 4)
    return np.ascontiguousarray(words), np.ascontiguousarray(byte.astype(np.uint8).reshape(k // 512, 16, n))


def unpack_weight(words, scales, fmt):
    g, p, n, _ = words.shape
    if fmt == "e4m3":
        vals = np.ascontiguousarray(words).view(ml_dtypes.float8_e4m3fn).astype(np.float64)
    else:
        nib = np.empty((g, p, n, 4), np.uint8)
        nib[..., 0::2] = words & 0xF
        nib[..., 1::2] = words >> 4
        vals = E2M1[nib]
    vals = vals * np.repeat(np.exp2(scales.astype(np.float64) - 127.0), 8, axis=1)[..., None]
    return vals.transpose(0, 1, 3, 2).reshape(g * 512, n)


B, S, C, H, D = 1, 256, 1024, 8, 1024
E = H * D
EPS = 1e-15
FMT = "e4m3"


def setup_inputs():
    t = mx_kscale(E)
    q_feat = bf(np.maximum(np.random.standard_normal((B, H, S, D)), 0.0))
    vk = bf(np.random.standard_normal((B, H, D, D)) * np.sqrt(S) * t.reshape(H, D)[None, :, :, None])
    k_sum = bf(S * (0.11 + 0.02 * np.random.standard_normal((B, H, D))))
    wo = np.random.standard_normal((C, E)) * 6.0 / np.sqrt(E) / t[None, :]
    words, scales = pack_weight(np.ascontiguousarray(wo.T), FMT)
    bo = bf(np.random.standard_normal(C) * 0.1)
    return {"q_feat": q_feat,
            "vk": vk,
            "k_sum": k_sum,
            "Wo_words": words,
            "Wo_scales": scales,
            "bo": bo}


def reference(q_feat, vk, k_sum, Wo_words, Wo_scales, bo):
    hs = f64(vk) @ f64(q_feat).transpose(0, 1, 3, 2)
    den = (f64(q_feat) * f64(k_sum)[:, :, None, :]).sum(-1)
    hs = hs / (den[:, :, None, :] + EPS)
    a = hs.transpose(0, 3, 1, 2).reshape(B, S, E)
    return (mxq(a, 2, "e4m3") @ unpack_weight(Wo_words, Wo_scales, FMT)) + f64(bo)

@@ -1,0 +1,290 @@
+from contextlib import ExitStack
+
+import concourse.mybir as mybir
+from concourse.masks import make_identity
+
+BF16 = mybir.dt.bfloat16
+F32 = mybir.dt.float32
+I32 = mybir.dt.int32
+U32 = mybir.dt.uint32
+U8 = mybir.dt.uint8
+FP8X4 = mybir.dt.float8_e4m3fn_x4
+COPY = mybir.ActivationFunctionType.Copy
+ADD = mybir.AluOpType.add
+
+P = 128
+HEADS = 8
+TOKENS = 256
+CHANNELS = 1024
+OUT_CHANNELS = 1024
+EPS = 1e-15
+
+PACK = 4
+K_PASS = P * PACK
+GROUPS_PER_HEAD = CHANNELS // K_PASS
+GROUPS = HEADS * GROUPS_PER_HEAD
+TOKEN_BLOCKS = TOKENS // P
+PAIR = 2
+WORD_BLOCKS = CHANNELS // PAIR // P
+BANK = 512
+FLIPS_PER_BANK = BANK // P
+OUT_HALVES = OUT_CHANNELS // BANK
+STEPS = WORD_BLOCKS * PAIR
+PLANES_PER_TILE = 4
+W_PIECES = HEADS
+W_PIECE_GROUPS = OUT_HALVES * GROUPS // W_PIECES
+
+VK_BUFS = 5
+Q_BUFS = 3
+SCALES_WITH_GROUP = GROUPS - VK_BUFS
+EARLY_PASSES = 4
+
+FLOPS = 2 * HEADS * TOKENS * CHANNELS * (CHANNELS + 1) + 2 * TOKENS * HEADS * CHANNELS * OUT_CHANNELS
+
+
+def tile_lineartransformerblock_pc_k_kernel(tc, q_feat, vk, k_sum, Wo_words, Wo_scales, bo, out):
+    nc = tc.nc
+    with ExitStack() as ctx:
+        keep = ctx.enter_context(tc.tile_pool(name="keep", bufs=1))
+        vk_pool = ctx.enter_context(tc.tile_pool(name="vk", bufs=VK_BUFS))
+        q_pool = ctx.enter_context(tc.tile_pool(name="q", bufs=Q_BUFS))
+        flipped_pool = ctx.enter_context(tc.tile_pool(name="flipped", bufs=2))
+        den_pool = ctx.enter_context(tc.tile_pool(name="den", bufs=3))
+        a_pool = ctx.enter_context(tc.tile_pool(name="a", bufs=3))
+        sums_pool = ctx.enter_context(tc.psum_pool(name="sums", bufs=2))
+        flip_pool = ctx.enter_context(tc.psum_pool(name="flip", bufs=6))
+        ctx.enter_context(tc.manual_schedule())
+
+        ident_words = keep.tile([P, P], F32)
+        ident_bf16 = keep.tile([P, P], BF16)
+        w_words = keep.tile([P, OUT_HALVES, GROUPS, BANK], U32, align_bytes=64)
+        w_planes = keep.tile([P, GROUPS // PLANES_PER_TILE, OUT_CHANNELS], U8, align_bytes=64)
+        a_words = keep.tile([P, GROUPS, TOKENS], U32, align_bytes=64)
+        a_planes = keep.tile([P, GROUPS, TOKENS], U8, align_bytes=64)
+        bias_rows = keep.tile([P, OUT_CHANNELS], BF16)
+        out_rows = keep.tile([P, TOKEN_BLOCKS, OUT_CHANNELS], F32)
+        table_warmer = keep.tile([P, 2], F32)
+        k_sum_rows = keep.tile([P, CHANNELS], BF16)
+        k_sum_flipped = keep.tile([P, WORD_BLOCKS * P], F32)
+
+        q_rows = {}
+        vk_rows = {}
+        q_flipped = {}
+        vk_flipped = {}
+        inv_den = {}
+        a_rows = {}
+        a_grouped = {}
+        open_bank = {}
+
+        def load_q(h):
+            rows = q_pool.tile([P, TOKEN_BLOCKS, CHANNELS], BF16, name="q_rows")
+            nc.sync.dma_start(out=rows[:], in_=q_feat[0, h].rearrange("(p b) d -> p b d", b=TOKEN_BLOCKS))
+            q_rows[h] = rows
+
+        def load_k_sum():
+            nc.sync.dma_start(out=k_sum_rows[0:HEADS, :], in_=k_sum[0])
+
+        def load_vk(g):
+            h, part = divmod(g, GROUPS_PER_HEAD)
+            rows = vk_pool.tile([P, PACK, CHANNELS], BF16, name="vk_rows")
+            nc.sync.dma_start(
+                out=rows[:],
+                in_=vk[0, h, part * K_PASS : (part + 1) * K_PASS, :].rearrange("(p t) d -> p t d", t=PACK),
+            )
+            vk_rows[g] = rows
+
+        def load_w_words(piece):
+            half, quarter = divmod(piece, W_PIECES // OUT_HALVES)
+            groups = slice(quarter * W_PIECE_GROUPS, (quarter + 1) * W_PIECE_GROUPS)
+            code_bytes = slice(half * BANK * PACK, (half + 1) * BANK * PACK)
+            nc.sync.dma_start(
+                out=w_words[:, half, groups, :].bitcast(I32),
+                in_=Wo_words[groups].rearrange("g p n t -> p g (n t)")[:, :, code_bytes].bitcast(I32),
+            )
+
+        def load_w_planes():
+            for i in range(GROUPS // PLANES_PER_TILE):
+                for quadrant in range(4):
+                    nc.sync.dma_start(
+                        out=w_planes[32 * quadrant : 32 * quadrant + 16, i, :].bitcast(I32),
+                        in_=Wo_scales[
+                            PLANES_PER_TILE * i : PLANES_PER_TILE * (i + 1), 4 * quadrant : 4 * quadrant + 4, :
+                        ].bitcast(I32),
+                    )
+
+        def flip_q(h, step):
+            j, b = divmod(step, TOKEN_BLOCKS)
+            place = step % FLIPS_PER_BANK
+            if step == 0:
+                flipped = flipped_pool.tile([P, WORD_BLOCKS * TOKEN_BLOCKS, PAIR, P], BF16, name="q_flipped")
+                q_flipped[h] = flipped
+            if place == 0:
+                bank = flip_pool.tile([P, BANK], F32, name="q_bank", tag="flip")
+                open_bank["q"] = bank
+            nc.tensor.transpose(
+                open_bank["q"][:, place * P : (place + 1) * P],
+                q_rows[h][:].bitcast(F32)[:, b, j * P : (j + 1) * P],
+                ident_words[:],
+            )
+            if place == FLIPS_PER_BANK - 1:
+                nc.vector.tensor_copy(
+                    out=q_flipped[h][:, step - place : step + 1, :, :],
+                    in_=open_bank["q"][:].bitcast(BF16).rearrange("w (x s e) -> w x e s", x=FLIPS_PER_BANK, e=PAIR),
+                )
+
+        def flip_k_sum():
+            bank = flip_pool.tile([P, BANK], F32, name="k_sum_bank", tag="flip")
+            for j in range(WORD_BLOCKS):
+                nc.tensor.transpose(
+                    bank[:, j * P : (j + 1) * P], k_sum_rows[:].bitcast(F32)[:, j * P : (j + 1) * P], ident_words[:]
+                )
+            nc.vector.tensor_copy(out=k_sum_flipped[:], in_=bank[:])
+
+        def flip_vk(g, step):
+            j, t = divmod(step, PACK)
+            if step == 0:
+                flipped = flipped_pool.tile([P, WORD_BLOCKS, BANK], F32, name="vk_flipped")
+                vk_flipped[g] = flipped
+            if t == 0:
+                bank = flip_pool.tile([P, BANK], F32, name="vk_bank", tag="flip")
+                open_bank["vk"] = bank
+            nc.tensor.transpose(
+                open_bank["vk"][:, t * P : (t + 1) * P],
+                vk_rows[g][:].bitcast(F32)[:, t, j * P : (j + 1) * P],
+                ident_words[:],
+            )
+            if t == PACK - 1:
+                nc.scalar.copy(out=vk_flipped[g][:, j, :], in_=open_bank["vk"][:])
+
+        def flip_a(g, step):
+            b, t = divmod(step, PACK)
+            if step == 0:
+                bank = flip_pool.tile([P, PACK, TOKENS], BF16, name="a_bank", tag="flip")
+                open_bank["a"] = bank
+            nc.tensor.transpose(
+                open_bank["a"][:, t, b * P : (b + 1) * P], a_rows[g][:, b, t * P : (t + 1) * P], ident_bf16[:]
+            )
+
+        def regroup(g):
+            grouped = a_pool.tile([P, TOKENS, PACK], BF16, name="a_grouped", align_bytes=64)
+            nc.vector.tensor_copy(out=grouped[:], in_=open_bank["a"][:].rearrange("p t s -> p s t"))
+            a_grouped[g] = grouped
+
+        def multiply(g, b, step, hs, den):
+            h, part = divmod(g, GROUPS_PER_HEAD)
+            j, e = divmod(step, PAIR)
+            tokens = q_flipped[h][:, j * TOKEN_BLOCKS + b, e, :]
+            values = vk_flipped[g][:].bitcast(BF16).rearrange("w j (c e) -> w j c e", e=PAIR)
+            key_sums = k_sum_flipped[:].bitcast(BF16).rearrange("w (j r e) -> w j r e", j=WORD_BLOCKS, e=PAIR)
+            nc.tensor.matmul(hs[:], lhsT=tokens, rhs=values[:, j, :, e], start=(step == 0), stop=(step == STEPS - 1))
+            if part == 0:
+                nc.tensor.matmul(
+                    den[:], lhsT=tokens, rhs=key_sums[:, j, h : h + 1, e], start=(step == 0), stop=(step == STEPS - 1)
+                )
+
+        def invert(h, b, den):
+            if b == 0:
+                inverse = den_pool.tile([P, TOKEN_BLOCKS], F32, name="inv_den")
+                inv_den[h] = inverse
+            guarded = den_pool.tile([P, 1], F32, name="guarded")
+            nc.vector.tensor_scalar_add(out=guarded[:], in0=den[:], scalar1=EPS)
+            nc.vector.reciprocal(out=inv_den[h][:, b : b + 1], in_=guarded[:])
+
+        def normalise(g, b, hs):
+            if b == 0:
+                rows = a_pool.tile([P, TOKEN_BLOCKS, K_PASS], BF16, name="a_rows")
+                a_rows[g] = rows
+            nc.scalar.activation(
+                out=a_rows[g][:, b, :], in_=hs[:], func=COPY, scale=inv_den[g // GROUPS_PER_HEAD][:, b : b + 1]
+            )
+
+        def quantise(g):
+            nc.vector.quantize_mx(
+                out=a_words[:, g, :].bitcast(FP8X4),
+                scales=a_planes[:, g, :],
+                in_=a_grouped[g][:].rearrange("p s t -> p (s t)"),
+            )
+
+        def project(sums, half, b, groups):
+            for g in groups:
+                i, k = divmod(g, PLANES_PER_TILE)
+                nc.tensor.matmul_mx(
+                    out=sums[:],
+                    lhsT=a_words[:, g, b * P : (b + 1) * P].bitcast(FP8X4),
+                    lhsT_scale=a_planes[:, g, b * P : (b + 1) * P],
+                    rhs=w_words[:, half, g, :].bitcast(FP8X4),
+                    rhs_scale=w_planes[PACK * k : P, i, half * BANK : (half + 1) * BANK],
+                    start=(g == 0),
+                    stop=(g == GROUPS - 1),
+                )
+
+        nc.vector.memset(k_sum_rows[:].bitcast(I32), 0)
+        load_q(0)
+        load_k_sum()
+        load_vk(0)
+        load_vk(1)
+        load_q(1)
+        for g in range(2, VK_BUFS):
+            load_vk(g)
+        for h in range(2, Q_BUFS):
+            load_q(h)
+
+        make_identity(nc, ident_words[:])
+        make_identity(nc, ident_bf16[:])
+        nc.vector.memset(w_planes[:].bitcast(I32), 0)
+        nc.vector.memset(table_warmer[:, 0:1], 0.0)
+        nc.scalar.activation(out=table_warmer[:, 1:2], in_=table_warmer[:, 0:1], func=COPY)
+
+        for step in range(WORD_BLOCKS * TOKEN_BLOCKS):
+            flip_q(0, step)
+        flip_k_sum()
+        for step in range(WORD_BLOCKS * PACK):
+            flip_vk(0, step)
+
+        for g in range(GROUPS):
+            h, part = divmod(g, GROUPS_PER_HEAD)
+            if g + VK_BUFS < GROUPS:
+                load_vk(g + VK_BUFS)
+            if part == 0 and h + Q_BUFS < HEADS:
+                load_q(h + Q_BUFS)
+            if part == 1:
+                load_w_words(h)
+            if g == SCALES_WITH_GROUP:
+                load_w_planes()
+                nc.sync.dma_start(out=bias_rows[:], in_=bo.partition_broadcast(P))
+
+            if g >= 2:
+                quantise(g - 2)
+
+            for b in range(TOKEN_BLOCKS):
+                hs = sums_pool.tile([P, BANK], F32, name="hs", tag="sums")
+                den = flip_pool.tile([P, 1], F32, name="den", tag="flip") if part == 0 else None
+                for step in range(STEPS):
+                    multiply(g, b, step, hs, den)
+                    if g + 1 < GROUPS:
+                        flip_vk(g + 1, b * STEPS + step)
+                    if b == 0 and part == 1 and h + 1 < HEADS:
+                        flip_q(h + 1, step)
+                    if b == 1 and g >= 1:
+                        flip_a(g - 1, step)
+                if part == 0:
+                    invert(h, b, den)
+                normalise(g, b, hs)
+            if g >= 1:
+                regroup(g - 1)
+
+        quantise(GROUPS - 2)
+        out_view = out[0].rearrange("(p b) c -> p b c", b=TOKEN_BLOCKS)
+        for half in range(OUT_HALVES):
+            columns = slice(half * BANK, (half + 1) * BANK)
+            for b in range(TOKEN_BLOCKS):
+                sums = sums_pool.tile([P, BANK], F32, name="out_sums", tag="sums")
+                project(sums, half, b, range(EARLY_PASSES))
+                if half == 0 and b == 0:
+                    for step in range(TOKEN_BLOCKS * PACK):
+                        flip_a(GROUPS - 1, step)
+                    regroup(GROUPS - 1)
+                    quantise(GROUPS - 1)
+                project(sums, half, b, range(EARLY_PASSES, GROUPS))
+                nc.vector.tensor_tensor(out=out_rows[:, b, columns], in0=sums[:], in1=bias_rows[:, columns], op=ADD)
+                nc.sync.dma_start(out=out_view[:, b, columns], in_=out_rows[:, b, columns])

@@ -25,6 +25,7 @@ GROUPS_PER_HEAD = CHANNELS // K_PASS
 GROUPS = HEADS * GROUPS_PER_HEAD
 TOKEN_BLOCKS = TOKENS // P
 PAIR = 2
+WORD_PAIRS = PACK // PAIR
 WORD_BLOCKS = CHANNELS // PAIR // P
 BANK = 512
 FLIPS_PER_BANK = BANK // P
@@ -56,7 +57,6 @@ def tile_lineartransformerblock_pc_k_kernel(tc, q_feat, vk, k_sum, Wo_words, Wo_
         ctx.enter_context(tc.manual_schedule())
 
         ident_words = keep.tile([P, P], F32)
-        ident_bf16 = keep.tile([P, P], BF16)
         w_words = keep.tile([P, OUT_HALVES, GROUPS, BANK], U32, align_bytes=64)
         w_planes = keep.tile([P, GROUPS // PLANES_PER_TILE, OUT_CHANNELS], U8, align_bytes=64)
         a_words = keep.tile([P, GROUPS, TOKENS], U32, align_bytes=64)
@@ -157,17 +157,22 @@ def tile_lineartransformerblock_pc_k_kernel(tc, q_feat, vk, k_sum, Wo_words, Wo_
                 nc.scalar.copy(out=vk_flipped[g][:, j, :], in_=open_bank["vk"][:])
 
         def flip_a(g, step):
-            b, t = divmod(step, PACK)
+            b, u = divmod(step, WORD_PAIRS)
             if step == 0:
-                bank = flip_pool.tile([P, PACK, TOKENS], BF16, name="a_bank", tag="flip")
+                bank = flip_pool.tile([P, WORD_PAIRS, TOKENS], F32, name="a_bank", tag="flip")
                 open_bank["a"] = bank
             nc.tensor.transpose(
-                open_bank["a"][:, t, b * P : (b + 1) * P], a_rows[g][:, b, t * P : (t + 1) * P], ident_bf16[:]
+                open_bank["a"][:, u, b * P : (b + 1) * P],
+                a_rows[g][:, b, :].bitcast(F32)[:, u * P : (u + 1) * P],
+                ident_words[:],
             )
 
         def regroup(g):
             grouped = a_pool.tile([P, TOKENS, PACK], BF16, name="a_grouped", align_bytes=64)
-            nc.vector.tensor_copy(out=grouped[:], in_=open_bank["a"][:].rearrange("p t s -> p s t"))
+            nc.vector.tensor_copy(
+                out=grouped[:].rearrange("p s t -> p (s t)").bitcast(F32).rearrange("p (s u) -> p s u", u=WORD_PAIRS),
+                in_=open_bank["a"][:].rearrange("p u s -> p s u"),
+            )
             a_grouped[g] = grouped
 
         def multiply(g, b, step, hs, den):
@@ -195,7 +200,10 @@ def tile_lineartransformerblock_pc_k_kernel(tc, q_feat, vk, k_sum, Wo_words, Wo_
                 rows = a_pool.tile([P, TOKEN_BLOCKS, K_PASS], BF16, name="a_rows")
                 a_rows[g] = rows
             nc.scalar.activation(
-                out=a_rows[g][:, b, :], in_=hs[:], func=COPY, scale=inv_den[g // GROUPS_PER_HEAD][:, b : b + 1]
+                out=a_rows[g][:, b, :].rearrange("s (u p e) -> s u p e", u=WORD_PAIRS, e=PAIR),
+                in_=hs[:].rearrange("s (u e p) -> s u p e", u=WORD_PAIRS, e=PAIR),
+                func=COPY,
+                scale=inv_den[g // GROUPS_PER_HEAD][:, b : b + 1],
             )
 
         def quantise(g):
@@ -230,7 +238,6 @@ def tile_lineartransformerblock_pc_k_kernel(tc, q_feat, vk, k_sum, Wo_words, Wo_
             load_q(h)
 
         make_identity(nc, ident_words[:])
-        make_identity(nc, ident_bf16[:])
         nc.vector.memset(w_planes[:].bitcast(I32), 0)
         nc.vector.memset(table_warmer[:, 0:1], 0.0)
         nc.scalar.activation(out=table_warmer[:, 1:2], in_=table_warmer[:, 0:1], func=COPY)
@@ -265,8 +272,8 @@ def tile_lineartransformerblock_pc_k_kernel(tc, q_feat, vk, k_sum, Wo_words, Wo_
                         flip_vk(g + 1, b * STEPS + step)
                     if b == 0 and part == 1 and h + 1 < HEADS:
                         flip_q(h + 1, step)
-                    if b == 1 and g >= 1:
-                        flip_a(g - 1, step)
+                    if b == 1 and g >= 1 and step % 2 == 0:
+                        flip_a(g - 1, step // 2)
                 if part == 0:
                     invert(h, b, den)
                 normalise(g, b, hs)
@@ -281,7 +288,7 @@ def tile_lineartransformerblock_pc_k_kernel(tc, q_feat, vk, k_sum, Wo_words, Wo_
                 sums = sums_pool.tile([P, BANK], F32, name="out_sums", tag="sums")
                 project(sums, half, b, range(EARLY_PASSES))
                 if half == 0 and b == 0:
-                    for step in range(TOKEN_BLOCKS * PACK):
+                    for step in range(TOKEN_BLOCKS * WORD_PAIRS):
                         flip_a(GROUPS - 1, step)
                     regroup(GROUPS - 1)
                     quantise(GROUPS - 1)

@@ -35,10 +35,15 @@ PLANES_PER_TILE = 4
 W_PIECES = HEADS
 W_PIECE_GROUPS = OUT_HALVES * GROUPS // W_PIECES
 
+FIRST_CHANNEL = 4
+K_SUM_COLUMN = FIRST_CHANNEL - 1
+HEAD_COLUMNS = FIRST_CHANNEL + CHANNELS
+PIECES = ((K_SUM_COLUMN, 344), (344, 688), (688, HEAD_COLUMNS))
+
 VK_BUFS = 5
 Q_BUFS = 3
-SCALES_WITH_GROUP = GROUPS - VK_BUFS
-EARLY_PASSES = 4
+NORMALISE_LAG = 3
+EARLY_PASSES = 6
 
 FLOPS = 2 * HEADS * TOKENS * CHANNELS * (CHANNELS + 1) + 2 * TOKENS * HEADS * CHANNELS * OUT_CHANNELS
 
@@ -51,9 +56,9 @@ def tile_lineartransformerblock_pc_k_kernel(tc, q_feat, vk, k_sum, Wo_words, Wo_
         q_pool = ctx.enter_context(tc.tile_pool(name="q", bufs=Q_BUFS))
         flipped_pool = ctx.enter_context(tc.tile_pool(name="flipped", bufs=2))
         den_pool = ctx.enter_context(tc.tile_pool(name="den", bufs=3))
-        a_pool = ctx.enter_context(tc.tile_pool(name="a", bufs=3))
-        sums_pool = ctx.enter_context(tc.psum_pool(name="sums", bufs=2))
-        flip_pool = ctx.enter_context(tc.psum_pool(name="flip", bufs=6))
+        a_pool = ctx.enter_context(tc.tile_pool(name="a", bufs=2))
+        sums_pool = ctx.enter_context(tc.psum_pool(name="sums", bufs=3))
+        flip_pool = ctx.enter_context(tc.psum_pool(name="flip", bufs=5))
         ctx.enter_context(tc.manual_schedule())
 
         ident_words = keep.tile([P, P], F32)
@@ -65,7 +70,7 @@ def tile_lineartransformerblock_pc_k_kernel(tc, q_feat, vk, k_sum, Wo_words, Wo_
         out_rows = keep.tile([P, TOKEN_BLOCKS, OUT_CHANNELS], F32)
         table_warmer = keep.tile([P, 2], F32)
         k_sum_rows = keep.tile([P, CHANNELS], BF16)
-        k_sum_flipped = keep.tile([P, WORD_BLOCKS * P], F32)
+        k_sum_flipped = keep.tile([P, WORD_BLOCKS, P], F32)
 
         q_rows = {}
         vk_rows = {}
@@ -133,18 +138,21 @@ def tile_lineartransformerblock_pc_k_kernel(tc, q_feat, vk, k_sum, Wo_words, Wo_
                 )
 
         def flip_k_sum():
-            bank = flip_pool.tile([P, BANK], F32, name="k_sum_bank", tag="flip")
+            bank = flip_pool.tile([P, WORD_BLOCKS, P], F32, name="k_sum_bank", tag="flip")
             for j in range(WORD_BLOCKS):
-                nc.tensor.transpose(
-                    bank[:, j * P : (j + 1) * P], k_sum_rows[:].bitcast(F32)[:, j * P : (j + 1) * P], ident_words[:]
-                )
+                nc.tensor.transpose(bank[:, j, :], k_sum_rows[:].bitcast(F32)[:, j * P : (j + 1) * P], ident_words[:])
             nc.vector.tensor_copy(out=k_sum_flipped[:], in_=bank[:])
 
+        def open_head(h):
+            flipped = flipped_pool.tile([P, WORD_BLOCKS, HEAD_COLUMNS], F32, name="vk_flipped")
+            vk_flipped[h] = flipped
+            nc.scalar.copy(out=flipped[:, :, K_SUM_COLUMN:FIRST_CHANNEL], in_=k_sum_flipped[:, :, h : h + 1])
+
         def flip_vk(g, step):
+            h, part = divmod(g, GROUPS_PER_HEAD)
             j, t = divmod(step, PACK)
-            if step == 0:
-                flipped = flipped_pool.tile([P, WORD_BLOCKS, BANK], F32, name="vk_flipped")
-                vk_flipped[g] = flipped
+            if part == 0 and step == 0:
+                open_head(h)
             if t == 0:
                 bank = flip_pool.tile([P, BANK], F32, name="vk_bank", tag="flip")
                 open_bank["vk"] = bank
@@ -154,63 +162,69 @@ def tile_lineartransformerblock_pc_k_kernel(tc, q_feat, vk, k_sum, Wo_words, Wo_
                 ident_words[:],
             )
             if t == PACK - 1:
-                nc.scalar.copy(out=vk_flipped[g][:, j, :], in_=open_bank["vk"][:])
-
-        def flip_a(g, step):
-            b, u = divmod(step, WORD_PAIRS)
-            if step == 0:
-                bank = flip_pool.tile([P, WORD_PAIRS, TOKENS], F32, name="a_bank", tag="flip")
-                open_bank["a"] = bank
-            nc.tensor.transpose(
-                open_bank["a"][:, u, b * P : (b + 1) * P],
-                a_rows[g][:, b, :].bitcast(F32)[:, u * P : (u + 1) * P],
-                ident_words[:],
-            )
-
-        def regroup(g):
-            grouped = a_pool.tile([P, TOKENS, PACK], BF16, name="a_grouped", align_bytes=64)
-            nc.vector.tensor_copy(
-                out=grouped[:].rearrange("p s t -> p (s t)").bitcast(F32).rearrange("p (s u) -> p s u", u=WORD_PAIRS),
-                in_=open_bank["a"][:].rearrange("p u s -> p s u"),
-            )
-            a_grouped[g] = grouped
-
-        def multiply(g, b, step, hs, den):
-            h, part = divmod(g, GROUPS_PER_HEAD)
-            j, e = divmod(step, PAIR)
-            tokens = q_flipped[h][:, j * TOKEN_BLOCKS + b, e, :]
-            values = vk_flipped[g][:].bitcast(BF16).rearrange("w j (c e) -> w j c e", e=PAIR)
-            key_sums = k_sum_flipped[:].bitcast(BF16).rearrange("w (j r e) -> w j r e", j=WORD_BLOCKS, e=PAIR)
-            nc.tensor.matmul(hs[:], lhsT=tokens, rhs=values[:, j, :, e], start=(step == 0), stop=(step == STEPS - 1))
-            if part == 0:
-                nc.tensor.matmul(
-                    den[:], lhsT=tokens, rhs=key_sums[:, j, h : h + 1, e], start=(step == 0), stop=(step == STEPS - 1)
+                first = FIRST_CHANNEL + part * K_PASS
+                nc.scalar.copy(
+                    out=vk_flipped[h][:, j, first : first + K_PASS].rearrange("w (u p e) -> w u p e", u=WORD_PAIRS, e=PAIR),
+                    in_=open_bank["vk"][:].rearrange("w (u e p) -> w u p e", u=WORD_PAIRS, e=PAIR),
                 )
 
-        def invert(h, b, den):
+        def flip_a(h, b, step):
+            part, u = divmod(step, WORD_PAIRS)
+            if step == 0:
+                bank = flip_pool.tile([P, GROUPS_PER_HEAD, WORD_PAIRS, P], F32, name="a_bank", tag="flip")
+                open_bank["a"] = bank
+                if b == 0:
+                    grouped = a_pool.tile([P, GROUPS_PER_HEAD, TOKENS, PACK], BF16, name="a_grouped", align_bytes=64)
+                    a_grouped[h] = grouped
+            block = GROUPS_PER_HEAD * part + u
+            nc.tensor.transpose(
+                open_bank["a"][:, part, u, :],
+                a_rows[h][:, b, :].bitcast(F32)[:, block * P : (block + 1) * P],
+                ident_words[:],
+            )
+            if step == FLIPS_PER_BANK - 1:
+                words = a_grouped[h][:].rearrange("p g s t -> p (g s t)").bitcast(F32)
+                words = words.rearrange("p (g s u) -> p g s u", g=GROUPS_PER_HEAD, u=WORD_PAIRS)
+                nc.vector.tensor_copy(
+                    out=words[:, :, b * P : (b + 1) * P, :], in_=open_bank["a"][:].rearrange("p g u s -> p g s u")
+                )
+
+        def multiply(h, b, columns, step, sums):
+            j, e = divmod(step, PAIR)
+            values = vk_flipped[h][:].bitcast(BF16).rearrange("w j (c e) -> w j c e", e=PAIR)
+            first, last = columns
+            nc.tensor.matmul(
+                sums[:, 0 : last - first],
+                lhsT=q_flipped[h][:, j * TOKEN_BLOCKS + b, e, :],
+                rhs=values[:, j, first:last, e],
+                start=(step == 0),
+                stop=(step == STEPS - 1),
+            )
+
+        def invert(h, b, sums):
             if b == 0:
                 inverse = den_pool.tile([P, TOKEN_BLOCKS], F32, name="inv_den")
                 inv_den[h] = inverse
             guarded = den_pool.tile([P, 1], F32, name="guarded")
-            nc.vector.tensor_scalar_add(out=guarded[:], in0=den[:], scalar1=EPS)
+            nc.vector.tensor_scalar_add(out=guarded[:], in0=sums[:, 0:1], scalar1=EPS)
             nc.vector.reciprocal(out=inv_den[h][:, b : b + 1], in_=guarded[:])
 
-        def normalise(g, b, hs):
-            if b == 0:
-                rows = a_pool.tile([P, TOKEN_BLOCKS, K_PASS], BF16, name="a_rows")
-                a_rows[g] = rows
+        def normalise(h, b, columns, sums):
+            first, last = columns
+            skip = 1 if first == K_SUM_COLUMN else 0
             nc.scalar.activation(
-                out=a_rows[g][:, b, :].rearrange("s (u p e) -> s u p e", u=WORD_PAIRS, e=PAIR),
-                in_=hs[:].rearrange("s (u e p) -> s u p e", u=WORD_PAIRS, e=PAIR),
+                out=a_rows[h][:, b, first + skip - FIRST_CHANNEL : last - FIRST_CHANNEL],
+                in_=sums[:, skip : last - first],
                 func=COPY,
-                scale=inv_den[g // GROUPS_PER_HEAD][:, b : b + 1],
+                scale=inv_den[h][:, b : b + 1],
             )
 
-        def quantise(g):
+        def quantise(h):
+            groups = slice(h * GROUPS_PER_HEAD, (h + 1) * GROUPS_PER_HEAD)
             nc.vector.quantize_mx(
-                out=a_words[:, g, :].bitcast(FP8X4),
-                scales=a_planes[:, g, :],
-                in_=a_grouped[g][:].rearrange("p s t -> p (s t)"),
+                out=a_words[:, groups, :].rearrange("p g s -> p (g s)").bitcast(FP8X4),
+                scales=a_planes[:, groups, :].rearrange("p g s -> p (g s)"),
+                in_=a_grouped[h][:].rearrange("p g s t -> p (g s t)"),
             )
 
         def project(sums, half, b, groups):
@@ -248,50 +262,94 @@ def tile_lineartransformerblock_pc_k_kernel(tc, q_feat, vk, k_sum, Wo_words, Wo_
         for step in range(WORD_BLOCKS * PACK):
             flip_vk(0, step)
 
-        for g in range(GROUPS):
-            h, part = divmod(g, GROUPS_PER_HEAD)
-            if g + VK_BUFS < GROUPS:
-                load_vk(g + VK_BUFS)
-            if part == 0 and h + Q_BUFS < HEADS:
-                load_q(h + Q_BUFS)
-            if part == 1:
-                load_w_words(h)
-            if g == SCALES_WITH_GROUP:
-                load_w_planes()
-                nc.sync.dma_start(out=bias_rows[:], in_=bo.partition_broadcast(P))
+        def q_bank(h, half):
+            return [lambda step=step: flip_q(h, step) for step in range(half * FLIPS_PER_BANK, (half + 1) * FLIPS_PER_BANK)]
 
-            if g >= 2:
-                quantise(g - 2)
+        def vk_bank(g, j):
+            return [lambda step=step: flip_vk(g, step) for step in range(j * PACK, (j + 1) * PACK)]
 
-            for b in range(TOKEN_BLOCKS):
-                hs = sums_pool.tile([P, BANK], F32, name="hs", tag="sums")
-                den = flip_pool.tile([P, 1], F32, name="den", tag="flip") if part == 0 else None
+        def vk_banks(g):
+            return [flip for j in range(WORD_BLOCKS) for flip in vk_bank(g, j)]
+
+        def a_bank(h, b):
+            return [lambda step=step: flip_a(h, b, step) for step in range(FLIPS_PER_BANK)]
+
+        waiting = []
+
+        def normalise_waiting():
+            for piece in waiting:
+                normalise(*piece)
+            waiting.clear()
+
+        def run_phase(h, units, flips):
+            slots = len(units) * STEPS
+            done = 0
+            for index, (columns, b) in enumerate(units):
+                sums = sums_pool.tile([P, BANK], F32, name="hs", tag="sums")
                 for step in range(STEPS):
-                    multiply(g, b, step, hs, den)
-                    if g + 1 < GROUPS:
-                        flip_vk(g + 1, b * STEPS + step)
-                    if b == 0 and part == 1 and h + 1 < HEADS:
-                        flip_q(h + 1, step)
-                    if b == 1 and g >= 1 and step % 2 == 0:
-                        flip_a(g - 1, step // 2)
-                if part == 0:
-                    invert(h, b, den)
-                normalise(g, b, hs)
-            if g >= 1:
-                regroup(g - 1)
+                    multiply(h, b, columns, step, sums)
+                    due = (index * STEPS + step + 1) * len(flips) // slots
+                    for flip in flips[done:due]:
+                        flip()
+                    done = due
+                    if step == NORMALISE_LAG:
+                        normalise_waiting()
+                if columns[0] == K_SUM_COLUMN:
+                    invert(h, b, sums)
+                waiting.append((h, b, columns, sums))
 
-        quantise(GROUPS - 2)
+        blocks = range(TOKEN_BLOCKS)
+        for h in range(HEADS):
+            rows = a_pool.tile([P, TOKEN_BLOCKS, CHANNELS], BF16, name="a_rows")
+            a_rows[h] = rows
+            if h + Q_BUFS < HEADS:
+                load_q(h + Q_BUFS)
+            if h == 0:
+                phases = [
+                    ([(PIECES[0], b) for b in blocks], vk_banks(1)),
+                    ([(PIECES[1], b) for b in blocks], vk_banks(2)),
+                    ([(PIECES[2], b) for b in blocks], q_bank(1, 0) + q_bank(1, 1) + vk_banks(3)),
+                ]
+            else:
+                phases = []
+                for b in blocks:
+                    flips = []
+                    if h + 1 < HEADS:
+                        flips = q_bank(h + 1, b) + vk_bank(GROUPS_PER_HEAD * (h + 1) + b, 0)
+                    if b == 0:
+                        if h == 1:
+                            flips = flips + a_bank(0, 0)
+                        flips = flips + a_bank(h - 1, TOKEN_BLOCKS - 1)
+                    else:
+                        flips = flips + a_bank(h, b - 1)
+                    if h + 1 < HEADS:
+                        for j in range(1, WORD_BLOCKS):
+                            flips = flips + vk_bank(GROUPS_PER_HEAD * (h + 1) + b, j)
+                    phases.append(([(columns, b) for columns in PIECES], flips))
+            for index, (units, flips) in enumerate(phases):
+                next_group = len(vk_rows)
+                if next_group < GROUPS:
+                    load_vk(next_group)
+                if index == len(phases) - 1:
+                    load_w_words(h)
+                    if h == HEADS - 2:
+                        load_w_planes()
+                        nc.sync.dma_start(out=bias_rows[:], in_=bo.partition_broadcast(P))
+                run_phase(h, units, flips)
+                if h > 0 and index == 0:
+                    quantise(h - 1)
+        normalise_waiting()
+
         out_view = out[0].rearrange("(p b) c -> p b c", b=TOKEN_BLOCKS)
         for half in range(OUT_HALVES):
             columns = slice(half * BANK, (half + 1) * BANK)
-            for b in range(TOKEN_BLOCKS):
+            for b in blocks:
                 sums = sums_pool.tile([P, BANK], F32, name="out_sums", tag="sums")
                 project(sums, half, b, range(EARLY_PASSES))
                 if half == 0 and b == 0:
-                    for step in range(TOKEN_BLOCKS * WORD_PAIRS):
-                        flip_a(GROUPS - 1, step)
-                    regroup(GROUPS - 1)
-                    quantise(GROUPS - 1)
+                    for flip in a_bank(HEADS - 1, TOKEN_BLOCKS - 1):
+                        flip()
+                    quantise(HEADS - 1)
                 project(sums, half, b, range(EARLY_PASSES, GROUPS))
                 nc.vector.tensor_tensor(out=out_rows[:, b, columns], in0=sums[:], in1=bias_rows[:, columns], op=ADD)
                 nc.sync.dma_start(out=out_view[:, b, columns], in_=out_rows[:, b, columns])

@@ -32,7 +32,7 @@ FLIPS_PER_BANK = BANK // P
 OUT_HALVES = OUT_CHANNELS // BANK
 STEPS = WORD_BLOCKS * PAIR
 PLANES_PER_TILE = 4
-W_PIECES = HEADS
+W_PIECES = 8
 W_PIECE_GROUPS = OUT_HALVES * GROUPS // W_PIECES
 
 FIRST_CHANNEL = 4
@@ -330,11 +330,11 @@ def tile_lineartransformerblock_pc_k_kernel(tc, q_feat, vk, k_sum, Wo_words, Wo_
                 next_group = len(vk_rows)
                 if next_group < GROUPS:
                     load_vk(next_group)
-                if index == len(phases) - 1:
-                    load_w_words(h)
-                    if h == HEADS - 2:
-                        load_w_planes()
-                        nc.sync.dma_start(out=bias_rows[:], in_=bo.partition_broadcast(P))
+                if next_group == GROUPS - 1:
+                    for piece in range(W_PIECES):
+                        load_w_words(piece)
+                    load_w_planes()
+                    nc.sync.dma_start(out=bias_rows[:], in_=bo.partition_broadcast(P))
                 run_phase(h, units, flips)
                 if h > 0 and index == 0:
                     quantise(h - 1)

@@ -39,6 +39,7 @@ FIRST_CHANNEL = 4
 K_SUM_COLUMN = FIRST_CHANNEL - 1
 HEAD_COLUMNS = FIRST_CHANNEL + CHANNELS
 PIECES = ((K_SUM_COLUMN, 344), (344, 688), (688, HEAD_COLUMNS))
+FIRST_PIECES = ((K_SUM_COLUMN, 260), (260, 516), (516, HEAD_COLUMNS))
 
 VK_BUFS = 5
 Q_BUFS = 3
@@ -69,8 +70,8 @@ def tile_lineartransformerblock_pc_k_kernel(tc, q_feat, vk, k_sum, Wo_words, Wo_
         bias_rows = keep.tile([P, OUT_CHANNELS], BF16)
         out_rows = keep.tile([P, TOKEN_BLOCKS, OUT_CHANNELS], F32)
         table_warmer = keep.tile([P, 2], F32)
-        k_sum_rows = keep.tile([P, CHANNELS], BF16)
-        k_sum_flipped = keep.tile([P, WORD_BLOCKS, P], F32)
+        k_sum_rows = keep.tile([P, PAIR * P], BF16)
+        k_sum_flipped = keep.tile([P, P], F32)
 
         q_rows = {}
         vk_rows = {}
@@ -79,24 +80,21 @@ def tile_lineartransformerblock_pc_k_kernel(tc, q_feat, vk, k_sum, Wo_words, Wo_
         inv_den = {}
         a_rows = {}
         a_grouped = {}
-        open_bank = {}
 
-        def load_q(h):
-            rows = q_pool.tile([P, TOKEN_BLOCKS, CHANNELS], BF16, name="q_rows")
-            nc.sync.dma_start(out=rows[:], in_=q_feat[0, h].rearrange("(p b) d -> p b d", b=TOKEN_BLOCKS))
-            q_rows[h] = rows
+        def load_q(h, blocks=slice(0, TOKEN_BLOCKS)):
+            if h not in q_rows:
+                rows = q_pool.tile([P, TOKEN_BLOCKS, CHANNELS], BF16, name="q_rows")
+                q_rows[h] = rows
+            tokens = q_feat[0, h].rearrange("(p b) d -> p b d", b=TOKEN_BLOCKS)
+            nc.sync.dma_start(out=q_rows[h][:, blocks, :], in_=tokens[:, blocks, :])
 
-        def load_k_sum():
-            nc.sync.dma_start(out=k_sum_rows[0:HEADS, :], in_=k_sum[0])
-
-        def load_vk(g):
+        def load_vk(g, ts=slice(0, PACK), ds=slice(0, CHANNELS)):
             h, part = divmod(g, GROUPS_PER_HEAD)
-            rows = vk_pool.tile([P, PACK, CHANNELS], BF16, name="vk_rows")
-            nc.sync.dma_start(
-                out=rows[:],
-                in_=vk[0, h, part * K_PASS : (part + 1) * K_PASS, :].rearrange("(p t) d -> p t d", t=PACK),
-            )
-            vk_rows[g] = rows
+            if g not in vk_rows:
+                rows = vk_pool.tile([P, PACK, CHANNELS], BF16, name="vk_rows")
+                vk_rows[g] = rows
+            channels = vk[0, h, part * K_PASS : (part + 1) * K_PASS, :].rearrange("(p t) d -> p t d", t=PACK)
+            nc.sync.dma_start(out=vk_rows[g][:, ts, ds], in_=channels[:, ts, ds])
 
         def load_w_words(piece):
             half, quarter = divmod(piece, W_PIECES // OUT_HALVES)
@@ -117,77 +115,96 @@ def tile_lineartransformerblock_pc_k_kernel(tc, q_feat, vk, k_sum, Wo_words, Wo_
                         ].bitcast(I32),
                     )
 
-        def flip_q(h, step):
-            j, b = divmod(step, TOKEN_BLOCKS)
-            place = step % FLIPS_PER_BANK
-            if step == 0:
-                flipped = flipped_pool.tile([P, WORD_BLOCKS * TOKEN_BLOCKS, PAIR, P], BF16, name="q_flipped")
-                q_flipped[h] = flipped
-            if place == 0:
-                bank = flip_pool.tile([P, BANK], F32, name="q_bank", tag="flip")
-                open_bank["q"] = bank
-            nc.tensor.transpose(
-                open_bank["q"][:, place * P : (place + 1) * P],
-                q_rows[h][:].bitcast(F32)[:, b, j * P : (j + 1) * P],
-                ident_words[:],
-            )
-            if place == FLIPS_PER_BANK - 1:
-                nc.vector.tensor_copy(
-                    out=q_flipped[h][:, step - place : step + 1, :, :],
-                    in_=open_bank["q"][:].bitcast(BF16).rearrange("w (x s e) -> w x e s", x=FLIPS_PER_BANK, e=PAIR),
+        def bank_of_flips(name, sources, copy_out):
+            opened = []
+
+            def flip(place):
+                if place == 0:
+                    bank = flip_pool.tile([P, len(sources) * P], F32, name=name, tag="flip")
+                    opened.append(bank)
+                nc.tensor.transpose(opened[0][:, place * P : (place + 1) * P], sources[place](), ident_words[:])
+                if place == len(sources) - 1:
+                    copy_out(opened[0][:])
+
+            return [lambda place=place: flip(place) for place in range(len(sources))]
+
+        def q_bank(h, b, js=range(WORD_BLOCKS), copy=nc.vector.tensor_copy):
+            def copy_out(bank):
+                if h not in q_flipped:
+                    flipped = flipped_pool.tile([P, WORD_BLOCKS, TOKEN_BLOCKS, PAIR, P], BF16, name="q_flipped")
+                    q_flipped[h] = flipped
+                copy(
+                    out=q_flipped[h][:, js[0] : js[0] + len(js), b, :, :],
+                    in_=bank.bitcast(BF16).rearrange("w (j s e) -> w j e s", j=len(js), e=PAIR),
                 )
+                if b == TOKEN_BLOCKS - 1 and h + Q_BUFS < HEADS:
+                    load_q(h + Q_BUFS)
+
+            sources = [lambda j=j: q_rows[h][:, b, :].bitcast(F32)[:, j * P : (j + 1) * P] for j in js]
+            return bank_of_flips("q_bank", sources, copy_out)
 
         def flip_k_sum():
-            bank = flip_pool.tile([P, WORD_BLOCKS, P], F32, name="k_sum_bank", tag="flip")
-            for j in range(WORD_BLOCKS):
-                nc.tensor.transpose(bank[:, j, :], k_sum_rows[:].bitcast(F32)[:, j * P : (j + 1) * P], ident_words[:])
+            bank = flip_pool.tile([P, P], F32, name="k_sum_bank", tag="flip")
+            nc.tensor.transpose(bank[:], k_sum_rows[:].bitcast(F32), ident_words[:])
             nc.vector.tensor_copy(out=k_sum_flipped[:], in_=bank[:])
 
         def open_head(h):
             flipped = flipped_pool.tile([P, WORD_BLOCKS, HEAD_COLUMNS], F32, name="vk_flipped")
             vk_flipped[h] = flipped
-            nc.scalar.copy(out=flipped[:, :, K_SUM_COLUMN:FIRST_CHANNEL], in_=k_sum_flipped[:, :, h : h + 1])
-
-        def flip_vk(g, step):
-            h, part = divmod(g, GROUPS_PER_HEAD)
-            j, t = divmod(step, PACK)
-            if part == 0 and step == 0:
-                open_head(h)
-            if t == 0:
-                bank = flip_pool.tile([P, BANK], F32, name="vk_bank", tag="flip")
-                open_bank["vk"] = bank
-            nc.tensor.transpose(
-                open_bank["vk"][:, t * P : (t + 1) * P],
-                vk_rows[g][:].bitcast(F32)[:, t, j * P : (j + 1) * P],
-                ident_words[:],
+            nc.scalar.copy(
+                out=flipped[:, :, K_SUM_COLUMN], in_=k_sum_flipped[:, h * WORD_BLOCKS : (h + 1) * WORD_BLOCKS]
             )
-            if t == PACK - 1:
-                first = FIRST_CHANNEL + part * K_PASS
-                nc.scalar.copy(
-                    out=vk_flipped[h][:, j, first : first + K_PASS].rearrange("w (u p e) -> w u p e", u=WORD_PAIRS, e=PAIR),
-                    in_=open_bank["vk"][:].rearrange("w (u e p) -> w u p e", u=WORD_PAIRS, e=PAIR),
-                )
 
-        def flip_a(h, b, step):
-            part, u = divmod(step, WORD_PAIRS)
-            if step == 0:
-                bank = flip_pool.tile([P, GROUPS_PER_HEAD, WORD_PAIRS, P], F32, name="a_bank", tag="flip")
-                open_bank["a"] = bank
+        def vk_bank(g, js, ts):
+            h, part = divmod(g, GROUPS_PER_HEAD)
+
+            def copy_out(bank):
+                if h not in vk_flipped:
+                    open_head(h)
+                first = FIRST_CHANNEL + part * K_PASS + ts[0] * P
+                last = first + len(ts) * P
+                if len(js) == 1:
+                    columns = vk_flipped[h][:, js[0], first:last].rearrange("w (u p e) -> w u p e", p=P, e=PAIR)
+                    bank = bank.rearrange("w (u e p) -> w u p e", p=P, e=PAIR)
+                else:
+                    columns = vk_flipped[h][:, js[0] : js[0] + len(js), first:last]
+                    columns = columns.rearrange("w j (p e) -> w j p e", e=PAIR)
+                    bank = bank.rearrange("w (j e p) -> w j p e", j=len(js), e=PAIR)
+                nc.scalar.copy(out=columns, in_=bank)
+                if js[-1] == WORD_BLOCKS - 1 and ts[-1] == PACK - 1:
+                    vk_is_flipped(g)
+
+            sources = [
+                lambda j=j, t=t: vk_rows[g][:, t, :].bitcast(F32)[:, j * P : (j + 1) * P] for j in js for t in ts
+            ]
+            return bank_of_flips("vk_bank", sources, copy_out)
+
+        def vk_is_flipped(g):
+            if g + VK_BUFS < GROUPS:
+                load_vk(g + VK_BUFS)
+            if g + VK_BUFS == GROUPS - 1:
+                for piece in range(W_PIECES):
+                    load_w_words(piece)
+                load_w_planes()
+                nc.sync.dma_start(out=bias_rows[:], in_=bo.partition_broadcast(P))
+
+        def a_bank(h, b):
+            def copy_out(bank):
                 if b == 0:
                     grouped = a_pool.tile([P, GROUPS_PER_HEAD, TOKENS, PACK], BF16, name="a_grouped", align_bytes=64)
                     a_grouped[h] = grouped
-            block = GROUPS_PER_HEAD * part + u
-            nc.tensor.transpose(
-                open_bank["a"][:, part, u, :],
-                a_rows[h][:, b, :].bitcast(F32)[:, block * P : (block + 1) * P],
-                ident_words[:],
-            )
-            if step == FLIPS_PER_BANK - 1:
                 words = a_grouped[h][:].rearrange("p g s t -> p (g s t)").bitcast(F32)
                 words = words.rearrange("p (g s u) -> p g s u", g=GROUPS_PER_HEAD, u=WORD_PAIRS)
                 nc.vector.tensor_copy(
-                    out=words[:, :, b * P : (b + 1) * P, :], in_=open_bank["a"][:].rearrange("p g u s -> p g s u")
+                    out=words[:, :, b * P : (b + 1) * P, :],
+                    in_=bank.rearrange("p (g u s) -> p g s u", g=GROUPS_PER_HEAD, u=WORD_PAIRS),
                 )
+
+            sources = [
+                lambda block=block: a_rows[h][:, b, :].bitcast(F32)[:, block * P : (block + 1) * P]
+                for block in range(GROUPS_PER_HEAD * WORD_PAIRS)
+            ]
+            return bank_of_flips("a_bank", sources, copy_out)
 
         def multiply(h, b, columns, step, sums):
             j, e = divmod(step, PAIR)
@@ -195,7 +212,7 @@ def tile_lineartransformerblock_pc_k_kernel(tc, q_feat, vk, k_sum, Wo_words, Wo_
             first, last = columns
             nc.tensor.matmul(
                 sums[:, 0 : last - first],
-                lhsT=q_flipped[h][:, j * TOKEN_BLOCKS + b, e, :],
+                lhsT=q_flipped[h][:, j, b, e, :],
                 rhs=values[:, j, first:last, e],
                 start=(step == 0),
                 stop=(step == STEPS - 1),
@@ -241,38 +258,41 @@ def tile_lineartransformerblock_pc_k_kernel(tc, q_feat, vk, k_sum, Wo_words, Wo_
                 )
 
         nc.vector.memset(k_sum_rows[:].bitcast(I32), 0)
-        load_q(0)
-        load_k_sum()
-        load_vk(0)
+        load_q(0, slice(0, 1))
+        nc.sync.dma_start(
+            out=k_sum_rows[0 : HEADS * WORD_BLOCKS, :], in_=k_sum[0].rearrange("h (j d) -> (h j) d", j=WORD_BLOCKS)
+        )
+        for half in range(2):
+            load_vk(0, slice(0, PAIR), slice(half * CHANNELS // 2, (half + 1) * CHANNELS // 2))
+        load_q(0, slice(1, TOKEN_BLOCKS))
+        load_vk(0, slice(PAIR, PACK))
         load_vk(1)
+        load_vk(2)
         load_q(1)
-        for g in range(2, VK_BUFS):
+        for g in range(3, VK_BUFS):
             load_vk(g)
         for h in range(2, Q_BUFS):
             load_q(h)
 
         make_identity(nc, ident_words[:])
-        nc.vector.memset(w_planes[:].bitcast(I32), 0)
         nc.vector.memset(table_warmer[:, 0:1], 0.0)
         nc.scalar.activation(out=table_warmer[:, 1:2], in_=table_warmer[:, 0:1], func=COPY)
+        nc.vector.memset(w_planes[:].bitcast(I32), 0)
 
-        for step in range(WORD_BLOCKS * TOKEN_BLOCKS):
-            flip_q(0, step)
+        all_rows = range(PACK)
+        row_pairs = (range(0, PAIR), range(PAIR, PACK))
+        word_block_pairs = (range(0, PAIR), range(PAIR, WORD_BLOCKS))
+
+        def make_now(flips):
+            for flip in flips:
+                flip()
+
         flip_k_sum()
-        for step in range(WORD_BLOCKS * PACK):
-            flip_vk(0, step)
-
-        def q_bank(h, half):
-            return [lambda step=step: flip_q(h, step) for step in range(half * FLIPS_PER_BANK, (half + 1) * FLIPS_PER_BANK)]
-
-        def vk_bank(g, j):
-            return [lambda step=step: flip_vk(g, step) for step in range(j * PACK, (j + 1) * PACK)]
-
-        def vk_banks(g):
-            return [flip for j in range(WORD_BLOCKS) for flip in vk_bank(g, j)]
-
-        def a_bank(h, b):
-            return [lambda step=step: flip_a(h, b, step) for step in range(FLIPS_PER_BANK)]
+        make_now(q_bank(0, 0, word_block_pairs[0]))
+        make_now(q_bank(0, 0, word_block_pairs[1], nc.scalar.copy))
+        for js in word_block_pairs:
+            make_now(vk_bank(0, js, row_pairs[0]))
+        make_now(q_bank(0, 1))
 
         waiting = []
 
@@ -281,75 +301,70 @@ def tile_lineartransformerblock_pc_k_kernel(tc, q_feat, vk, k_sum, Wo_words, Wo_
                 normalise(*piece)
             waiting.clear()
 
-        def run_phase(h, units, flips):
-            slots = len(units) * STEPS
+        def run_phase(h, columns, flips):
+            slots = TOKEN_BLOCKS * STEPS
             done = 0
-            for index, (columns, b) in enumerate(units):
+            for b in range(TOKEN_BLOCKS):
                 sums = sums_pool.tile([P, BANK], F32, name="hs", tag="sums")
                 for step in range(STEPS):
                     multiply(h, b, columns, step, sums)
-                    due = (index * STEPS + step + 1) * len(flips) // slots
-                    for flip in flips[done:due]:
-                        flip()
+                    due = (b * STEPS + step + 1) * len(flips) // slots
+                    make_now(flips[done:due])
                     done = due
-                    if step == NORMALISE_LAG:
+                    if step == (NORMALISE_LAG if waiting and waiting[0][2][0] == K_SUM_COLUMN else 0):
                         normalise_waiting()
                 if columns[0] == K_SUM_COLUMN:
                     invert(h, b, sums)
                 waiting.append((h, b, columns, sums))
 
-        blocks = range(TOKEN_BLOCKS)
+        def no_flips(count):
+            return [lambda: None] * count
+
         for h in range(HEADS):
             rows = a_pool.tile([P, TOKEN_BLOCKS, CHANNELS], BF16, name="a_rows")
             a_rows[h] = rows
-            if h + Q_BUFS < HEADS:
-                load_q(h + Q_BUFS)
+            phases = [[], [], []]
             if h == 0:
-                phases = [
-                    ([(PIECES[0], b) for b in blocks], vk_banks(1)),
-                    ([(PIECES[1], b) for b in blocks], vk_banks(2)),
-                    ([(PIECES[2], b) for b in blocks], q_bank(1, 0) + q_bank(1, 1) + vk_banks(3)),
-                ]
-            else:
-                phases = []
-                for b in blocks:
-                    flips = []
-                    if h + 1 < HEADS:
-                        flips = q_bank(h + 1, b) + vk_bank(GROUPS_PER_HEAD * (h + 1) + b, 0)
-                    if b == 0:
-                        if h == 1:
-                            flips = flips + a_bank(0, 0)
-                        flips = flips + a_bank(h - 1, TOKEN_BLOCKS - 1)
-                    else:
-                        flips = flips + a_bank(h, b - 1)
-                    if h + 1 < HEADS:
-                        for j in range(1, WORD_BLOCKS):
-                            flips = flips + vk_bank(GROUPS_PER_HEAD * (h + 1) + b, j)
-                    phases.append(([(columns, b) for columns in PIECES], flips))
-            for index, (units, flips) in enumerate(phases):
-                next_group = len(vk_rows)
-                if next_group < GROUPS:
-                    load_vk(next_group)
-                if next_group == GROUPS - 1:
-                    for piece in range(W_PIECES):
-                        load_w_words(piece)
-                    load_w_planes()
-                    nc.sync.dma_start(out=bias_rows[:], in_=bo.partition_broadcast(P))
-                run_phase(h, units, flips)
-                if h > 0 and index == 0:
-                    quantise(h - 1)
+                late = [flip for js in word_block_pairs for flip in vk_bank(0, js, row_pairs[1])]
+                phases[0] = no_flips(len(late) // 2) + late + no_flips(len(late) // 2)
+            for j in range(WORD_BLOCKS):
+                second = vk_bank(GROUPS_PER_HEAD * h + 1, range(j, j + 1), all_rows)
+                phases[1 if h == 0 else 0].extend(second)
+            for b in range(TOKEN_BLOCKS):
+                flips = phases[2 if h == 0 else b + 1]
+                halves = word_block_pairs[b]
+                if h + 1 < HEADS:
+                    flips.extend(q_bank(h + 1, b))
+                    flips.extend(vk_bank(GROUPS_PER_HEAD * (h + 1), halves[0:1], all_rows))
+                if h > 0:
+                    flips.extend(a_bank(h - 1, b))
+                if h == HEADS - 1 and b == TOKEN_BLOCKS - 1:
+                    flips.extend(no_flips(2 * FLIPS_PER_BANK))
+                    flips.extend(a_bank(h, 0))
+                if h + 1 < HEADS:
+                    flips.extend(vk_bank(GROUPS_PER_HEAD * (h + 1), halves[1:2], all_rows))
+            for columns, flips in zip(FIRST_PIECES if h == 0 else PIECES, phases):
+                run_phase(h, columns, flips)
+            if h > 0:
+                quantise(h - 1)
         normalise_waiting()
 
         out_view = out[0].rearrange("(p b) c -> p b c", b=TOKEN_BLOCKS)
+
+        def finish(sums, half, b, columns):
+            stored = slice(half * BANK + columns.start, half * BANK + columns.stop)
+            nc.vector.tensor_tensor(
+                out=out_rows[:, b, stored], in0=sums[:, columns], in1=bias_rows[:, stored], op=ADD
+            )
+            nc.sync.dma_start(out=out_view[:, b, stored], in_=out_rows[:, b, stored])
+
         for half in range(OUT_HALVES):
-            columns = slice(half * BANK, (half + 1) * BANK)
-            for b in blocks:
+            for b in range(TOKEN_BLOCKS):
                 sums = sums_pool.tile([P, BANK], F32, name="out_sums", tag="sums")
                 project(sums, half, b, range(EARLY_PASSES))
                 if half == 0 and b == 0:
-                    for flip in a_bank(HEADS - 1, TOKEN_BLOCKS - 1):
-                        flip()
+                    make_now(a_bank(HEADS - 1, TOKEN_BLOCKS - 1))
                     quantise(HEADS - 1)
                 project(sums, half, b, range(EARLY_PASSES, GROUPS))
-                nc.vector.tensor_tensor(out=out_rows[:, b, columns], in0=sums[:], in1=bias_rows[:, columns], op=ADD)
-                nc.sync.dma_start(out=out_view[:, b, columns], in_=out_rows[:, b, columns])
+                for columns in (slice(0, BANK // 2), slice(BANK // 2, BANK)):
+                    finish(sums, half, b, columns)

@@ -44,6 +44,7 @@ FIRST_PIECES = ((K_SUM_COLUMN, 260), (260, 516), (516, HEAD_COLUMNS))
 VK_BUFS = 5
 Q_BUFS = 3
 NORMALISE_LAG = 3
+WARM_UPS = 4
 EARLY_PASSES = 6
 
 FLOPS = 2 * HEADS * TOKENS * CHANNELS * (CHANNELS + 1) + 2 * TOKENS * HEADS * CHANNELS * OUT_CHANNELS
@@ -70,6 +71,7 @@ def tile_lineartransformerblock_pc_k_kernel(tc, q_feat, vk, k_sum, Wo_words, Wo_
         bias_rows = keep.tile([P, OUT_CHANNELS], BF16)
         out_rows = keep.tile([P, TOKEN_BLOCKS, OUT_CHANNELS], F32)
         table_warmer = keep.tile([P, 2], F32)
+        warm_up = keep.tile([P, BANK], BF16)
         k_sum_rows = keep.tile([P, PAIR * P], BF16)
         k_sum_flipped = keep.tile([P, P], F32)
 
@@ -170,7 +172,10 @@ def tile_lineartransformerblock_pc_k_kernel(tc, q_feat, vk, k_sum, Wo_words, Wo_
                     columns = vk_flipped[h][:, js[0] : js[0] + len(js), first:last]
                     columns = columns.rearrange("w j (p e) -> w j p e", e=PAIR)
                     bank = bank.rearrange("w (j e p) -> w j p e", j=len(js), e=PAIR)
-                nc.scalar.copy(out=columns, in_=bank)
+                if js[-1] % 2 == 1 and len(js) == 1:
+                    nc.vector.tensor_copy(out=columns, in_=bank)
+                else:
+                    nc.scalar.copy(out=columns, in_=bank)
                 if js[-1] == WORD_BLOCKS - 1 and ts[-1] == PACK - 1:
                     vk_is_flipped(g)
 
@@ -257,6 +262,7 @@ def tile_lineartransformerblock_pc_k_kernel(tc, q_feat, vk, k_sum, Wo_words, Wo_
                     stop=(g == GROUPS - 1),
                 )
 
+        nc.vector.memset(warm_up[:].bitcast(I32), 0)
         nc.vector.memset(k_sum_rows[:].bitcast(I32), 0)
         load_q(0, slice(0, 1))
         nc.sync.dma_start(
@@ -287,6 +293,9 @@ def tile_lineartransformerblock_pc_k_kernel(tc, q_feat, vk, k_sum, Wo_words, Wo_
             for flip in flips:
                 flip()
 
+        for i in range(WARM_UPS):
+            idle = sums_pool.tile([P, BANK], F32, name="idle", tag="sums")
+            nc.tensor.matmul(idle[:], lhsT=warm_up[:, 0:P], rhs=warm_up[:], start=True, stop=True)
         flip_k_sum()
         make_now(q_bank(0, 0, word_block_pairs[0]))
         make_now(q_bank(0, 0, word_block_pairs[1], nc.scalar.copy))
@@ -333,11 +342,15 @@ def tile_lineartransformerblock_pc_k_kernel(tc, q_feat, vk, k_sum, Wo_words, Wo_
             for b in range(TOKEN_BLOCKS):
                 flips = phases[2 if h == 0 else b + 1]
                 halves = word_block_pairs[b]
+                if h == 0:
+                    vk_flips = [flip for j in halves for flip in vk_bank(GROUPS_PER_HEAD, range(j, j + 1), all_rows)]
+                    q_flips = q_bank(1, b)
+                    flips.extend(vk_flips + q_flips if b == 0 else q_flips + vk_flips)
+                    continue
                 if h + 1 < HEADS:
                     flips.extend(q_bank(h + 1, b))
                     flips.extend(vk_bank(GROUPS_PER_HEAD * (h + 1), halves[0:1], all_rows))
-                if h > 0:
-                    flips.extend(a_bank(h - 1, b))
+                flips.extend(a_bank(h - 1, b))
                 if h == HEADS - 1 and b == TOKEN_BLOCKS - 1:
                     flips.extend(no_flips(2 * FLIPS_PER_BANK))
                     flips.extend(a_bank(h, 0))

@@ -44,6 +44,7 @@ FIRST_PIECES = ((K_SUM_COLUMN, 260), (260, 516), (516, HEAD_COLUMNS))
 VK_BUFS = 5
 Q_BUFS = 3
 NORMALISE_LAG = 3
+FLIP_RUN = 2
 WARM_UPS = 4
 EARLY_PASSES = 6
 
@@ -317,7 +318,8 @@ def tile_lineartransformerblock_pc_k_kernel(tc, q_feat, vk, k_sum, Wo_words, Wo_
                 sums = sums_pool.tile([P, BANK], F32, name="hs", tag="sums")
                 for step in range(STEPS):
                     multiply(h, b, columns, step, sums)
-                    due = (b * STEPS + step + 1) * len(flips) // slots
+                    ended = (b * STEPS + step + 1) // FLIP_RUN * FLIP_RUN
+                    due = ended * len(flips) // slots
                     make_now(flips[done:due])
                     done = due
                     if step == (NORMALISE_LAG if waiting and waiting[0][2][0] == K_SUM_COLUMN else 0):

from contextlib import ExitStack

import concourse.mybir as mybir
from concourse.masks import make_identity

BF16 = mybir.dt.bfloat16
F32 = mybir.dt.float32
I32 = mybir.dt.int32
U32 = mybir.dt.uint32
U8 = mybir.dt.uint8
FP8X4 = mybir.dt.float8_e4m3fn_x4
COPY = mybir.ActivationFunctionType.Copy
ADD = mybir.AluOpType.add

P = 128
HEADS = 8
TOKENS = 256
CHANNELS = 1024
OUT_CHANNELS = 1024
EPS = 1e-15

PACK = 4
K_PASS = P * PACK
GROUPS_PER_HEAD = CHANNELS // K_PASS
GROUPS = HEADS * GROUPS_PER_HEAD
TOKEN_BLOCKS = TOKENS // P
PAIR = 2
WORD_PAIRS = PACK // PAIR
WORD_BLOCKS = CHANNELS // PAIR // P
BANK = 512
FLIPS_PER_BANK = BANK // P
OUT_HALVES = OUT_CHANNELS // BANK
STEPS = WORD_BLOCKS * PAIR
PLANES_PER_TILE = 4
W_PIECES = 8
W_PIECE_GROUPS = OUT_HALVES * GROUPS // W_PIECES

FIRST_CHANNEL = 4
K_SUM_COLUMN = FIRST_CHANNEL - 1
HEAD_COLUMNS = FIRST_CHANNEL + CHANNELS
PIECES = ((K_SUM_COLUMN, 344), (344, 688), (688, HEAD_COLUMNS))
FIRST_PIECES = ((K_SUM_COLUMN, 260), (260, 516), (516, HEAD_COLUMNS))

VK_BUFS = 5
Q_BUFS = 3
NORMALISE_LAG = 3
FLIP_RUN = 2
WARM_UPS = 4
EARLY_PASSES = 6

FLOPS = 2 * HEADS * TOKENS * CHANNELS * (CHANNELS + 1) + 2 * TOKENS * HEADS * CHANNELS * OUT_CHANNELS


def tile_lineartransformerblock_pc_k_kernel(tc, q_feat, vk, k_sum, Wo_words, Wo_scales, bo, out):
    nc = tc.nc
    with ExitStack() as ctx:
        keep = ctx.enter_context(tc.tile_pool(name="keep", bufs=1))
        vk_pool = ctx.enter_context(tc.tile_pool(name="vk", bufs=VK_BUFS))
        q_pool = ctx.enter_context(tc.tile_pool(name="q", bufs=Q_BUFS))
        flipped_pool = ctx.enter_context(tc.tile_pool(name="flipped", bufs=2))
        den_pool = ctx.enter_context(tc.tile_pool(name="den", bufs=3))
        a_pool = ctx.enter_context(tc.tile_pool(name="a", bufs=2))
        sums_pool = ctx.enter_context(tc.psum_pool(name="sums", bufs=3))
        flip_pool = ctx.enter_context(tc.psum_pool(name="flip", bufs=5))
        ctx.enter_context(tc.manual_schedule())

        ident_words = keep.tile([P, P], F32)
        w_words = keep.tile([P, OUT_HALVES, GROUPS, BANK], U32, align_bytes=64)
        w_planes = keep.tile([P, GROUPS // PLANES_PER_TILE, OUT_CHANNELS], U8, align_bytes=64)
        a_words = keep.tile([P, GROUPS, TOKENS], U32, align_bytes=64)
        a_planes = keep.tile([P, GROUPS, TOKENS], U8, align_bytes=64)
        bias_rows = keep.tile([P, OUT_CHANNELS], BF16)
        out_rows = keep.tile([P, TOKEN_BLOCKS, OUT_CHANNELS], F32)
        table_warmer = keep.tile([P, 2], F32)
        warm_up = keep.tile([P, BANK], BF16)
        k_sum_rows = keep.tile([P, PAIR * P], BF16)
        k_sum_flipped = keep.tile([P, P], F32)

        q_rows = {}
        vk_rows = {}
        q_flipped = {}
        vk_flipped = {}
        inv_den = {}
        a_rows = {}
        a_grouped = {}

        def load_q(h, blocks=slice(0, TOKEN_BLOCKS)):
            if h not in q_rows:
                rows = q_pool.tile([P, TOKEN_BLOCKS, CHANNELS], BF16, name="q_rows")
                q_rows[h] = rows
            tokens = q_feat[0, h].rearrange("(p b) d -> p b d", b=TOKEN_BLOCKS)
            nc.sync.dma_start(out=q_rows[h][:, blocks, :], in_=tokens[:, blocks, :])

        def load_vk(g, ts=slice(0, PACK), ds=slice(0, CHANNELS)):
            h, part = divmod(g, GROUPS_PER_HEAD)
            if g not in vk_rows:
                rows = vk_pool.tile([P, PACK, CHANNELS], BF16, name="vk_rows")
                vk_rows[g] = rows
            channels = vk[0, h, part * K_PASS : (part + 1) * K_PASS, :].rearrange("(p t) d -> p t d", t=PACK)
            nc.sync.dma_start(out=vk_rows[g][:, ts, ds], in_=channels[:, ts, ds])

        def load_w_words(piece):
            half, quarter = divmod(piece, W_PIECES // OUT_HALVES)
            groups = slice(quarter * W_PIECE_GROUPS, (quarter + 1) * W_PIECE_GROUPS)
            code_bytes = slice(half * BANK * PACK, (half + 1) * BANK * PACK)
            nc.sync.dma_start(
                out=w_words[:, half, groups, :].bitcast(I32),
                in_=Wo_words[groups].rearrange("g p n t -> p g (n t)")[:, :, code_bytes].bitcast(I32),
            )

        def load_w_planes():
            for i in range(GROUPS // PLANES_PER_TILE):
                for quadrant in range(4):
                    nc.sync.dma_start(
                        out=w_planes[32 * quadrant : 32 * quadrant + 16, i, :].bitcast(I32),
                        in_=Wo_scales[
                            PLANES_PER_TILE * i : PLANES_PER_TILE * (i + 1), 4 * quadrant : 4 * quadrant + 4, :
                        ].bitcast(I32),
                    )

        def bank_of_flips(name, sources, copy_out):
            opened = []

            def flip(place):
                if place == 0:
                    bank = flip_pool.tile([P, len(sources) * P], F32, name=name, tag="flip")
                    opened.append(bank)
                nc.tensor.transpose(opened[0][:, place * P : (place + 1) * P], sources[place](), ident_words[:])
                if place == len(sources) - 1:
                    copy_out(opened[0][:])

            return [lambda place=place: flip(place) for place in range(len(sources))]

        def q_bank(h, b, js=range(WORD_BLOCKS), copy=nc.vector.tensor_copy):
            def copy_out(bank):
                if h not in q_flipped:
                    flipped = flipped_pool.tile([P, WORD_BLOCKS, TOKEN_BLOCKS, PAIR, P], BF16, name="q_flipped")
                    q_flipped[h] = flipped
                copy(
                    out=q_flipped[h][:, js[0] : js[0] + len(js), b, :, :],
                    in_=bank.bitcast(BF16).rearrange("w (j s e) -> w j e s", j=len(js), e=PAIR),
                )
                if b == TOKEN_BLOCKS - 1 and h + Q_BUFS < HEADS:
                    load_q(h + Q_BUFS)

            sources = [lambda j=j: q_rows[h][:, b, :].bitcast(F32)[:, j * P : (j + 1) * P] for j in js]
            return bank_of_flips("q_bank", sources, copy_out)

        def flip_k_sum():
            bank = flip_pool.tile([P, P], F32, name="k_sum_bank", tag="flip")
            nc.tensor.transpose(bank[:], k_sum_rows[:].bitcast(F32), ident_words[:])
            nc.vector.tensor_copy(out=k_sum_flipped[:], in_=bank[:])

        def open_head(h):
            flipped = flipped_pool.tile([P, WORD_BLOCKS, HEAD_COLUMNS], F32, name="vk_flipped")
            vk_flipped[h] = flipped
            nc.scalar.copy(
                out=flipped[:, :, K_SUM_COLUMN], in_=k_sum_flipped[:, h * WORD_BLOCKS : (h + 1) * WORD_BLOCKS]
            )

        def vk_bank(g, js, ts):
            h, part = divmod(g, GROUPS_PER_HEAD)

            def copy_out(bank):
                if h not in vk_flipped:
                    open_head(h)
                first = FIRST_CHANNEL + part * K_PASS + ts[0] * P
                last = first + len(ts) * P
                if len(js) == 1:
                    columns = vk_flipped[h][:, js[0], first:last].rearrange("w (u p e) -> w u p e", p=P, e=PAIR)
                    bank = bank.rearrange("w (u e p) -> w u p e", p=P, e=PAIR)
                else:
                    columns = vk_flipped[h][:, js[0] : js[0] + len(js), first:last]
                    columns = columns.rearrange("w j (p e) -> w j p e", e=PAIR)
                    bank = bank.rearrange("w (j e p) -> w j p e", j=len(js), e=PAIR)
                if js[-1] % 2 == 1 and len(js) == 1:
                    nc.vector.tensor_copy(out=columns, in_=bank)
                else:
                    nc.scalar.copy(out=columns, in_=bank)
                if js[-1] == WORD_BLOCKS - 1 and ts[-1] == PACK - 1:
                    vk_is_flipped(g)

            sources = [
                lambda j=j, t=t: vk_rows[g][:, t, :].bitcast(F32)[:, j * P : (j + 1) * P] for j in js for t in ts
            ]
            return bank_of_flips("vk_bank", sources, copy_out)

        def vk_is_flipped(g):
            if g + VK_BUFS < GROUPS:
                load_vk(g + VK_BUFS)
            if g + VK_BUFS == GROUPS - 1:
                for piece in range(W_PIECES):
                    load_w_words(piece)
                load_w_planes()
                nc.sync.dma_start(out=bias_rows[:], in_=bo.partition_broadcast(P))

        def a_bank(h, b):
            def copy_out(bank):
                if b == 0:
                    grouped = a_pool.tile([P, GROUPS_PER_HEAD, TOKENS, PACK], BF16, name="a_grouped", align_bytes=64)
                    a_grouped[h] = grouped
                words = a_grouped[h][:].rearrange("p g s t -> p (g s t)").bitcast(F32)
                words = words.rearrange("p (g s u) -> p g s u", g=GROUPS_PER_HEAD, u=WORD_PAIRS)
                nc.vector.tensor_copy(
                    out=words[:, :, b * P : (b + 1) * P, :],
                    in_=bank.rearrange("p (g u s) -> p g s u", g=GROUPS_PER_HEAD, u=WORD_PAIRS),
                )

            sources = [
                lambda block=block: a_rows[h][:, b, :].bitcast(F32)[:, block * P : (block + 1) * P]
                for block in range(GROUPS_PER_HEAD * WORD_PAIRS)
            ]
            return bank_of_flips("a_bank", sources, copy_out)

        def multiply(h, b, columns, step, sums):
            j, e = divmod(step, PAIR)
            values = vk_flipped[h][:].bitcast(BF16).rearrange("w j (c e) -> w j c e", e=PAIR)
            first, last = columns
            nc.tensor.matmul(
                sums[:, 0 : last - first],
                lhsT=q_flipped[h][:, j, b, e, :],
                rhs=values[:, j, first:last, e],
                start=(step == 0),
                stop=(step == STEPS - 1),
            )

        def invert(h, b, sums):
            if b == 0:
                inverse = den_pool.tile([P, TOKEN_BLOCKS], F32, name="inv_den")
                inv_den[h] = inverse
            guarded = den_pool.tile([P, 1], F32, name="guarded")
            nc.vector.tensor_scalar_add(out=guarded[:], in0=sums[:, 0:1], scalar1=EPS)
            nc.vector.reciprocal(out=inv_den[h][:, b : b + 1], in_=guarded[:])

        def normalise(h, b, columns, sums):
            first, last = columns
            skip = 1 if first == K_SUM_COLUMN else 0
            nc.scalar.activation(
                out=a_rows[h][:, b, first + skip - FIRST_CHANNEL : last - FIRST_CHANNEL],
                in_=sums[:, skip : last - first],
                func=COPY,
                scale=inv_den[h][:, b : b + 1],
            )

        def quantise(h):
            groups = slice(h * GROUPS_PER_HEAD, (h + 1) * GROUPS_PER_HEAD)
            nc.vector.quantize_mx(
                out=a_words[:, groups, :].rearrange("p g s -> p (g s)").bitcast(FP8X4),
                scales=a_planes[:, groups, :].rearrange("p g s -> p (g s)"),
                in_=a_grouped[h][:].rearrange("p g s t -> p (g s t)"),
            )

        def project(sums, half, b, groups):
            for g in groups:
                i, k = divmod(g, PLANES_PER_TILE)
                nc.tensor.matmul_mx(
                    out=sums[:],
                    lhsT=a_words[:, g, b * P : (b + 1) * P].bitcast(FP8X4),
                    lhsT_scale=a_planes[:, g, b * P : (b + 1) * P],
                    rhs=w_words[:, half, g, :].bitcast(FP8X4),
                    rhs_scale=w_planes[PACK * k : P, i, half * BANK : (half + 1) * BANK],
                    start=(g == 0),
                    stop=(g == GROUPS - 1),
                )

        nc.vector.memset(warm_up[:].bitcast(I32), 0)
        nc.vector.memset(k_sum_rows[:].bitcast(I32), 0)
        load_q(0, slice(0, 1))
        nc.sync.dma_start(
            out=k_sum_rows[0 : HEADS * WORD_BLOCKS, :], in_=k_sum[0].rearrange("h (j d) -> (h j) d", j=WORD_BLOCKS)
        )
        for half in range(2):
            load_vk(0, slice(0, PAIR), slice(half * CHANNELS // 2, (half + 1) * CHANNELS // 2))
        load_q(0, slice(1, TOKEN_BLOCKS))
        load_vk(0, slice(PAIR, PACK))
        load_vk(1)
        load_vk(2)
        load_q(1)
        for g in range(3, VK_BUFS):
            load_vk(g)
        for h in range(2, Q_BUFS):
            load_q(h)

        make_identity(nc, ident_words[:])
        nc.vector.memset(table_warmer[:, 0:1], 0.0)
        nc.scalar.activation(out=table_warmer[:, 1:2], in_=table_warmer[:, 0:1], func=COPY)
        nc.vector.memset(w_planes[:].bitcast(I32), 0)

        all_rows = range(PACK)
        row_pairs = (range(0, PAIR), range(PAIR, PACK))
        word_block_pairs = (range(0, PAIR), range(PAIR, WORD_BLOCKS))

        def make_now(flips):
            for flip in flips:
                flip()

        for i in range(WARM_UPS):
            idle = sums_pool.tile([P, BANK], F32, name="idle", tag="sums")
            nc.tensor.matmul(idle[:], lhsT=warm_up[:, 0:P], rhs=warm_up[:], start=True, stop=True)
        flip_k_sum()
        make_now(q_bank(0, 0, word_block_pairs[0]))
        make_now(q_bank(0, 0, word_block_pairs[1], nc.scalar.copy))
        for js in word_block_pairs:
            make_now(vk_bank(0, js, row_pairs[0]))
        make_now(q_bank(0, 1))

        waiting = []

        def normalise_waiting():
            for piece in waiting:
                normalise(*piece)
            waiting.clear()

        def run_phase(h, columns, flips):
            slots = TOKEN_BLOCKS * STEPS
            done = 0
            for b in range(TOKEN_BLOCKS):
                sums = sums_pool.tile([P, BANK], F32, name="hs", tag="sums")
                for step in range(STEPS):
                    multiply(h, b, columns, step, sums)
                    ended = (b * STEPS + step + 1) // FLIP_RUN * FLIP_RUN
                    due = ended * len(flips) // slots
                    make_now(flips[done:due])
                    done = due
                    if step == (NORMALISE_LAG if waiting and waiting[0][2][0] == K_SUM_COLUMN else 0):
                        normalise_waiting()
                if columns[0] == K_SUM_COLUMN:
                    invert(h, b, sums)
                waiting.append((h, b, columns, sums))

        def no_flips(count):
            return [lambda: None] * count

        for h in range(HEADS):
            rows = a_pool.tile([P, TOKEN_BLOCKS, CHANNELS], BF16, name="a_rows")
            a_rows[h] = rows
            phases = [[], [], []]
            if h == 0:
                late = [flip for js in word_block_pairs for flip in vk_bank(0, js, row_pairs[1])]
                phases[0] = no_flips(len(late) // 2) + late + no_flips(len(late) // 2)
            for j in range(WORD_BLOCKS):
                second = vk_bank(GROUPS_PER_HEAD * h + 1, range(j, j + 1), all_rows)
                phases[1 if h == 0 else 0].extend(second)
            for b in range(TOKEN_BLOCKS):
                flips = phases[2 if h == 0 else b + 1]
                halves = word_block_pairs[b]
                if h == 0:
                    vk_flips = [flip for j in halves for flip in vk_bank(GROUPS_PER_HEAD, range(j, j + 1), all_rows)]
                    q_flips = q_bank(1, b)
                    flips.extend(vk_flips + q_flips if b == 0 else q_flips + vk_flips)
                    continue
                if h + 1 < HEADS:
                    flips.extend(q_bank(h + 1, b))
                    flips.extend(vk_bank(GROUPS_PER_HEAD * (h + 1), halves[0:1], all_rows))
                flips.extend(a_bank(h - 1, b))
                if h == HEADS - 1 and b == TOKEN_BLOCKS - 1:
                    flips.extend(no_flips(2 * FLIPS_PER_BANK))
                    flips.extend(a_bank(h, 0))
                if h + 1 < HEADS:
                    flips.extend(vk_bank(GROUPS_PER_HEAD * (h + 1), halves[1:2], all_rows))
            for columns, flips in zip(FIRST_PIECES if h == 0 else PIECES, phases):
                run_phase(h, columns, flips)
            if h > 0:
                quantise(h - 1)
        normalise_waiting()

        out_view = out[0].rearrange("(p b) c -> p b c", b=TOKEN_BLOCKS)

        def finish(sums, half, b, columns):
            stored = slice(half * BANK + columns.start, half * BANK + columns.stop)
            nc.vector.tensor_tensor(
                out=out_rows[:, b, stored], in0=sums[:, columns], in1=bias_rows[:, stored], op=ADD
            )
            nc.sync.dma_start(out=out_view[:, b, stored], in_=out_rows[:, b, stored])

        for half in range(OUT_HALVES):
            for b in range(TOKEN_BLOCKS):
                sums = sums_pool.tile([P, BANK], F32, name="out_sums", tag="sums")
                project(sums, half, b, range(EARLY_PASSES))
                if half == 0 and b == 0:
                    make_now(a_bank(HEADS - 1, TOKEN_BLOCKS - 1))
                    quantise(HEADS - 1)
                project(sums, half, b, range(EARLY_PASSES, GROUPS))
                for columns in (slice(0, BANK // 2), slice(BANK // 2, BANK)):
                    finish(sums, half, b, columns)
